import numpy as np
import ml_dtypes


def mxq(x, axis, fmt="e4m3"):
    dtype, down = {"e4m3": (ml_dtypes.float8_e4m3fn, 7), "e5m2": (ml_dtypes.float8_e5m2, 14)}[fmt]
    v = np.moveaxis(np.asarray(x, np.float32).astype(ml_dtypes.bfloat16).astype(np.float64), axis, -1)
    blocks = v.reshape(v.shape[:-1] + (-1, 32))
    amax = np.abs(blocks).max(-1, keepdims=True)
    byte = np.maximum(np.where(amax > 0, np.frexp(amax)[1] - 1 + 127, 0) - down, 1)
    scale = np.exp2(byte - 127.0)
    codes = (blocks / scale).astype(np.float32).astype(dtype).astype(np.float64)
    return np.moveaxis((codes * scale).reshape(v.shape), -1, axis)


WIDE = False


def mx_kscale(k):
    if not WIDE:
        return np.ones(k)
    levels = np.array([10, -10, 5, -5, 0])
    a = np.random.permutation(np.resize(levels, k // 512 * 4)).reshape(k // 512, 4)
    idx = np.arange(k)
    return np.exp2(a[idx // 512, idx % 128 // 32])


BF16 = ml_dtypes.bfloat16


def bf(x):
    return np.asarray(x, np.float32).astype(BF16)


def f64(x):
    return np.asarray(x).astype(np.float64)


B, C, H, W = 128, 1024, 3, 3
C3, P = 3 * C, H * W
EPS = 1e-5


def setup_inputs():
    s = mx_kscale(C3)
    n = np.random.standard_normal
    return {
        "fv": bf(n((B, C3, H, W)) * s[None, :, None, None]),
        "ft": bf(n((B, C))),
        "W1": bf(n((C, C3)) / np.sqrt(C3) / s[None, :]),
        "b1": bf(n(C) * 0.3),
        "g1": bf(1.0 + 0.1 * n(C)),
        "be1": bf(n(C) * 0.3),
        "m1": bf(n(C) * 0.3),
        "v1": bf(np.random.uniform(0.5, 1.5, C)),
        "Wfc1": bf(n((C, C)) * 0.7 / np.sqrt(C)),
        "bfc1": bf(n(C) * 0.3),
    }


def reference(fv, ft, W1, b1, g1, be1, m1, v1, Wfc1, bfc1):
    x = (mxq(f64(W1), 1, "e4m3") @ mxq(f64(fv).reshape(B, C3, P), 1, "e4m3")) + f64(b1)[None, :, None]
    s = f64(g1) / np.sqrt(f64(v1) + EPS)
    fv1 = np.maximum(x * s[None, :, None] + (f64(be1) - f64(m1) * s)[None, :, None], 0.0)
    ft1 = f64(ft) @ f64(Wfc1).T + f64(bfc1)
    out = fv1 + fv1 * ft1[:, :, None]
    return out.reshape(B, C, H, W)

@@ -1,0 +1,295 @@
+from contextlib import ExitStack
+
+import concourse.mybir as mybir
+from concourse.masks import make_identity
+
+F32 = mybir.dt.float32
+BF16 = mybir.dt.bfloat16
+U32 = mybir.dt.uint32
+U8 = mybir.dt.uint8
+FP8X4 = mybir.dt.float8_e4m3fn_x4
+ACT = mybir.ActivationFunctionType
+ALU = mybir.AluOpType
+
+P = 128
+B = 128
+C = 1024
+C3 = 3072
+PIX = 9
+GROUPS = 6
+OT = 8
+COLS = PIX * B
+EPS = 1e-5
+FLOPS = 2 * C * C3 * COLS + 2 * B * C * C
+
+
+def slot_of(pix):
+    if pix == 8:
+        return 8
+    return (pix % 2) * 4 + pix // 2
+
+
+def tile_joint_module_pa_kernel(tc, fv, ft, W1, b1, g1, be1, m1, v1, Wfc1, bfc1, out):
+    nc = tc.nc
+    with ExitStack() as ctx:
+        const = ctx.enter_context(tc.tile_pool(name="const", bufs=1))
+        keep = ctx.enter_context(tc.tile_pool(name="keep", bufs=1))
+        stage = ctx.enter_context(tc.tile_pool(name="stage", bufs=2))
+        psum = ctx.enter_context(tc.psum_pool(name="psum", bufs=8))
+
+        fv_flat = fv.rearrange("b c h w -> b (c h w)")
+        out_flat = out.rearrange("b o h w -> b (o h w)")
+        wfc_view = Wfc1.rearrange("(t p) k -> p t k", p=P)
+
+        ptile = const.tile([P, P], BF16)
+        nc.vector.memset(ptile[:], 0.0)
+        bt = const.tile([P, C], BF16)
+        nc.vector.memset(bt[:], 0.0)
+        ones = const.tile([P, P], BF16)
+        nc.vector.memset(ones[:], 1.0)
+        for v, vec in enumerate((b1, g1, be1, m1, v1)):
+            nc.scalar.dma_start(out=ptile[8 * v : 8 * v + 8, :], in_=vec.rearrange("(t p) -> t p", p=P))
+        nc.scalar.dma_start(out=bt[0:1, :], in_=bfc1.rearrange("(a n) -> a n", a=1))
+        ftraw = const.tile([P, C], BF16)
+        nc.scalar.dma_start(out=ftraw[:], in_=ft)
+        ident_f = const.tile([P, P], F32)
+        make_identity(nc, ident_f[:])
+        ident_b = const.tile([P, P], BF16)
+        make_identity(nc, ident_b[:])
+
+        fvc = keep.tile([P, GROUPS, COLS], U32, align_bytes=64)
+        fvs = keep.tile([P, GROUPS, COLS], U8, align_bytes=64)
+        w1c = keep.tile([P, OT, GROUPS * P], U32, align_bytes=64)
+        w1s = keep.tile([P, OT, GROUPS * P], U8, align_bytes=64)
+        wfcT = keep.tile([P, 4 * C], F32)
+        ftT = keep.tile([P, 4 * B], F32)
+        gate = keep.tile([P, C], F32)
+
+        fvraw = {}
+        wraw = {}
+        wfraw = {}
+
+        def load_fv(g):
+            raw = stage.tile([P, 512 * PIX], BF16, tag="fvraw", bufs=3, name="fvraw%d" % g)
+            nc.sync.dma_start(out=raw[:], in_=fv_flat[:, g * 4608 : (g + 1) * 4608])
+            fvraw[g] = raw
+
+        def load_w(ot):
+            raw = stage.tile([P, C3], BF16, tag="wraw", bufs=3, name="wraw%d" % ot)
+            nc.sync.dma_start(out=raw[:], in_=W1[ot * P : (ot + 1) * P, :])
+            wraw[ot] = raw
+
+        def load_wf(i):
+            raw = stage.tile([P, 2, C], BF16, tag="wfraw", bufs=2, name="wfraw%d" % i)
+            nc.sync.dma_start(out=raw[:], in_=wfc_view[:, 2 * i : 2 * i + 2, :])
+            wfraw[i] = raw
+
+        def fv_group(g):
+            words = fvraw[g][:].bitcast(F32).rearrange("b (u p m) -> b u p m", u=2, p=P, m=PIX)
+            tsb = stage.tile([P, 2560], F32, tag="tsb", bufs=2, name="tsb%d" % g)
+            tw = tsb[:].rearrange("p (m b u) -> p m b u", m=10, b=B, u=2)
+            for m0 in range(0, PIX, 2):
+                nm = min(2, PIX - m0)
+                bank = psum.tile([P, 2, 2, B], F32, tag="bank", name="fvbank")
+                for mm in range(nm):
+                    for u in range(2):
+                        nc.tensor.transpose(bank[:, mm, u, :], words[:, u, :, m0 + mm], ident_f[:])
+                nc.scalar.copy(
+                    out=tw[:, m0 : m0 + nm, :, :],
+                    in_=bank[:, 0:nm, :, :].rearrange("p m u b -> p m b u"),
+                )
+            fb = tsb[:].bitcast(BF16)
+            gr = stage.tile([P, PIX * 512], BF16, tag="gr", bufs=2, align_bytes=64, name="gr%d" % g)
+            grv = gr[:].rearrange("p (q j a) -> p q j a", q=PIX, j=256, a=2)
+            even = (
+                fb[:, 0:4098]
+                .rearrange("p (a c) -> p a c", a=2)[:, :, 0:2048]
+                .rearrange("p a (n j h) -> p a n j h", n=4, j=256, h=2)[:, :, :, :, 0]
+                .rearrange("p a n j -> p n j a")
+            )
+            odd = (
+                fb[:, 1:5119]
+                .rearrange("p (a c) -> p a c", a=2)[:, :, 0:2048]
+                .rearrange("p a (n j h) -> p a n j h", n=4, j=256, h=2)[:, :, :, :, 0]
+                .rearrange("p a n j -> p n j a")
+            )
+            last = (
+                fb[:, 512:4610]
+                .rearrange("p (a c) -> p a c", a=2)[:, :, 1536:2048]
+                .rearrange("p a (j h) -> p a j h", j=256, h=2)[:, :, :, 0]
+                .rearrange("p a j -> p j a")
+            )
+            nc.vector.tensor_copy(out=grv[:, 0:4, :, :], in_=even)
+            nc.vector.tensor_copy(out=grv[:, 4:8, :, :], in_=odd)
+            nc.vector.tensor_copy(out=grv[:, 8, :, :], in_=last)
+            return gr
+
+        def fv_quant(g, gr):
+            nc.vector.quantize_mx(
+                out=fvc[:, g, 0:1024].bitcast(FP8X4), scales=fvs[:, g, 0:1024], in_=gr[:, 0:4096]
+            )
+            nc.vector.quantize_mx(
+                out=fvc[:, g, 1024:1152].bitcast(FP8X4), scales=fvs[:, g, 1024:1152], in_=gr[:, 4096:4608]
+            )
+
+        def w_tile(ot):
+            words = wraw[ot][:].bitcast(F32)
+            wgr = stage.tile([P, C3], BF16, tag="wgr", bufs=2, align_bytes=64, name="wgr%d" % ot)
+            wv = wgr[:].bitcast(F32).rearrange("p (g o u) -> p g o u", g=GROUPS, o=P, u=2)
+            for g0 in range(0, GROUPS, 2):
+                bank = psum.tile([P, 2, 2, P], F32, tag="bank", name="wbank")
+                for gg in range(2):
+                    for u in range(2):
+                        k0 = 256 * (g0 + gg) + 128 * u
+                        nc.tensor.transpose(bank[:, gg, u, :], words[:, k0 : k0 + 128], ident_f[:])
+                nc.scalar.copy(
+                    out=wv[:, g0 : g0 + 2, :, :], in_=bank[:].rearrange("p g u o -> p g o u")
+                )
+            return wgr
+
+        def w_quant(ot, wgr):
+            nc.vector.quantize_mx(
+                out=w1c[:, ot, 0:512].bitcast(FP8X4), scales=w1s[:, ot, 0:512], in_=wgr[:, 0:2048]
+            )
+            nc.vector.quantize_mx(
+                out=w1c[:, ot, 512:768].bitcast(FP8X4), scales=w1s[:, ot, 512:768], in_=wgr[:, 2048:3072]
+            )
+
+        def params():
+            pbank = psum.tile([P, P], BF16, tag="bank", name="pbank")
+            nc.tensor.transpose(pbank[:], ptile[:], ident_b[:])
+            prm = const.tile([P, 40], F32)
+            nc.vector.tensor_copy(out=prm[:], in_=pbank[:, 0:40])
+            s_t = const.tile([P, OT], F32)
+            t_t = const.tile([P, OT], F32)
+            tmp = const.tile([P, OT], F32)
+            nc.vector.tensor_scalar_add(out=tmp[:], in0=prm[:, 32:40], scalar1=EPS)
+            nc.scalar.sqrt(out=tmp[:], in_=tmp[:])
+            nc.vector.reciprocal(out=tmp[:], in_=tmp[:])
+            nc.vector.tensor_mul(out=s_t[:], in0=prm[:, 8:16], in1=tmp[:])
+            nc.vector.tensor_sub(out=t_t[:], in0=prm[:, 0:8], in1=prm[:, 24:32])
+            nc.vector.tensor_mul(out=t_t[:], in0=t_t[:], in1=s_t[:])
+            nc.vector.tensor_add(out=t_t[:], in0=t_t[:], in1=prm[:, 16:24])
+            return s_t, t_t
+
+        def ft_transposes():
+            words = ftraw[:].bitcast(F32)
+            bank = psum.tile([P, 4, B], F32, tag="bank", name="ftbank")
+            for kc in range(4):
+                nc.tensor.transpose(bank[:, kc, :], words[:, kc * P : (kc + 1) * P], ident_f[:])
+            nc.scalar.copy(out=ftT[:], in_=bank[:].rearrange("p k b -> p (k b)"))
+
+        def wfc_half(h):
+            for kc in range(4):
+                bank = psum.tile([P, 4, P], F32, tag="bank", name="wfbank")
+                for i in range(4):
+                    ot = 4 * h + i
+                    words = wfraw[ot // 2][:, ot % 2, :].bitcast(F32)
+                    nc.tensor.transpose(bank[:, i, :], words[:, kc * P : (kc + 1) * P], ident_f[:])
+                nc.scalar.copy(
+                    out=wfcT[:, kc * C + h * 512 : kc * C + (h + 1) * 512],
+                    in_=bank[:].rearrange("p i o -> p (i o)"),
+                )
+
+        def gate_half(h):
+            wv = wfcT[:].bitcast(BF16).rearrange("p (k o e) -> p k o e", k=4, o=C, e=2)
+            fvw = ftT[:].bitcast(BF16).rearrange("p (k b e) -> p k b e", k=4, b=B, e=2)
+            acc = psum.tile([P, 512], F32, tag="bank", name="gbank")
+            for kc in range(4):
+                for e in range(2):
+                    nc.tensor.matmul(
+                        acc[:],
+                        lhsT=fvw[:, kc, :, e],
+                        rhs=wv[:, kc, h * 512 : (h + 1) * 512, e],
+                        start=(kc == 0 and e == 0),
+                        stop=False,
+                    )
+            nc.tensor.matmul(acc[:], lhsT=ones[:], rhs=bt[:, h * 512 : (h + 1) * 512], start=False, stop=True)
+            nc.vector.tensor_scalar_add(out=gate[:, h * 512 : (h + 1) * 512], in0=acc[:], scalar1=1.0)
+
+        CHUNKS = ((0, 512), (512, 512), (1024, 128))
+
+        def conv(ot, s_t, t_t):
+            y = stage.tile([P, COLS], F32, tag="y", bufs=2, name="y%d" % ot)
+            for c0, n in CHUNKS:
+                acc = psum.tile([P, n], F32, tag="bank", name="acc")
+                for g in range(GROUPS):
+                    nc.tensor.matmul_mx(
+                        out=acc[:],
+                        lhsT=w1c[:, ot, g * P : (g + 1) * P].bitcast(FP8X4),
+                        lhsT_scale=w1s[:, ot, g * P : (g + 1) * P],
+                        rhs=fvc[:, g, c0 : c0 + n].bitcast(FP8X4),
+                        rhs_scale=fvs[:, g, c0 : c0 + n],
+                        start=(g == 0),
+                        stop=(g == GROUPS - 1),
+                    )
+                nc.scalar.activation(
+                    out=y[:, c0 : c0 + n],
+                    in_=acc[:],
+                    func=ACT.Relu,
+                    bias=t_t[:, ot : ot + 1],
+                    scale=s_t[:, ot : ot + 1],
+                )
+            return y
+
+        def finish(ot, y):
+            planes = stage.tile([P, PIX, P], F32, tag="planes", bufs=2, name="planes%d" % ot)
+            for x0 in range(0, PIX, 4):
+                nx = min(4, PIX - x0)
+                z = psum.tile([P, nx, P], F32, tag="bank", name="z")
+                for i in range(nx):
+                    q = slot_of(x0 + i)
+                    nc.tensor.transpose(z[:, i, :], y[:, q * B : (q + 1) * B], ident_f[:])
+                nc.scalar.copy(out=planes[:, x0 : x0 + nx, :], in_=z[:])
+            osb = stage.tile([P, P, PIX], F32, tag="osb", bufs=3, name="osb%d" % ot)
+            nc.vector.tensor_tensor(
+                out=osb[:],
+                in0=planes[:].rearrange("b x o -> b o x"),
+                in1=gate[:, ot * P : (ot + 1) * P].unsqueeze(2).to_broadcast([P, P, PIX]),
+                op=ALU.mult,
+            )
+            nc.sync.dma_start(
+                out=out_flat[:, ot * COLS : (ot + 1) * COLS], in_=osb[:].rearrange("b o x -> b (o x)")
+            )
+
+        load_fv(0)
+        load_fv(1)
+        load_w(0)
+        load_fv(2)
+        prev = None
+        extra = {0: lambda: load_w(1), 1: lambda: load_wf(0), 2: lambda: load_wf(1)}
+        for g in range(GROUPS):
+            gr = fv_group(g)
+            if g == 0:
+                s_t, t_t = params()
+                ft_transposes()
+            if g + 3 < GROUPS:
+                load_fv(g + 3)
+                extra[g]()
+            if prev is not None:
+                fv_quant(g - 1, prev)
+            prev = gr
+        wgr0 = w_tile(0)
+        fv_quant(GROUPS - 1, prev)
+        w_quant(0, wgr0)
+        load_w(2)
+        wgr1 = w_tile(1)
+        w_quant(1, wgr1)
+        wfc_half(0)
+        load_wf(2)
+        load_wf(3)
+        gate_half(0)
+        ys = {}
+        for ot in range(OT):
+            ys[ot] = conv(ot, s_t, t_t)
+            if ot + 3 < OT:
+                load_w(ot + 3)
+            if ot + 2 < OT:
+                wgr = w_tile(ot + 2)
+                w_quant(ot + 2, wgr)
+            if ot == 0:
+                wfc_half(1)
+                gate_half(1)
+            if ot >= 1:
+                finish(ot - 1, ys[ot - 1])
+        finish(OT - 1, ys[OT - 1])

@@ -252,44 +252,45 @@ def tile_joint_module_pa_kernel(tc, fv, ft, W1, b1, g1, be1, m1, v1, Wfc1, bfc1,
                 out=out_flat[:, ot * COLS : (ot + 1) * COLS], in_=osb[:].rearrange("b o x -> b (o x)")
             )
 
-        load_fv(0)
-        load_fv(1)
-        load_w(0)
-        load_fv(2)
-        prev = None
-        extra = {0: lambda: load_w(1), 1: lambda: load_wf(0), 2: lambda: load_wf(1)}
-        for g in range(GROUPS):
-            gr = fv_group(g)
-            if g == 0:
-                s_t, t_t = params()
-                ft_transposes()
-            if g + 3 < GROUPS:
-                load_fv(g + 3)
-                extra[g]()
-            if prev is not None:
-                fv_quant(g - 1, prev)
-            prev = gr
-        wgr0 = w_tile(0)
-        fv_quant(GROUPS - 1, prev)
-        w_quant(0, wgr0)
-        load_w(2)
-        wgr1 = w_tile(1)
-        w_quant(1, wgr1)
-        wfc_half(0)
-        load_wf(2)
-        load_wf(3)
-        gate_half(0)
-        ys = {}
-        for ot in range(OT):
-            ys[ot] = conv(ot, s_t, t_t)
-            if ot + 3 < OT:
-                load_w(ot + 3)
-            if ot + 2 < OT:
-                wgr = w_tile(ot + 2)
-                w_quant(ot + 2, wgr)
-            if ot == 0:
-                wfc_half(1)
-                gate_half(1)
-            if ot >= 1:
-                finish(ot - 1, ys[ot - 1])
-        finish(OT - 1, ys[OT - 1])
+        with tc.manual_schedule():
+            load_fv(0)
+            load_fv(1)
+            load_w(0)
+            load_fv(2)
+            prev = None
+            extra = {0: lambda: load_w(1), 1: lambda: load_wf(0), 2: lambda: load_wf(1)}
+            for g in range(GROUPS):
+                gr = fv_group(g)
+                if g == 0:
+                    s_t, t_t = params()
+                    ft_transposes()
+                if g + 3 < GROUPS:
+                    load_fv(g + 3)
+                    extra[g]()
+                if prev is not None:
+                    fv_quant(g - 1, prev)
+                prev = gr
+            wgr0 = w_tile(0)
+            fv_quant(GROUPS - 1, prev)
+            w_quant(0, wgr0)
+            load_w(2)
+            wgr1 = w_tile(1)
+            w_quant(1, wgr1)
+            wfc_half(0)
+            load_wf(2)
+            load_wf(3)
+            gate_half(0)
+            ys = {}
+            for ot in range(OT):
+                ys[ot] = conv(ot, s_t, t_t)
+                if ot + 3 < OT:
+                    load_w(ot + 3)
+                if ot + 2 < OT:
+                    wgr = w_tile(ot + 2)
+                    w_quant(ot + 2, wgr)
+                if ot == 0:
+                    wfc_half(1)
+                    gate_half(1)
+                if ot >= 1:
+                    finish(ot - 1, ys[ot - 1])
+            finish(OT - 1, ys[OT - 1])

@@ -52,6 +52,9 @@ def tile_joint_module_pa_kernel(tc, fv, ft, W1, b1, g1, be1, m1, v1, Wfc1, bfc1,
         nc.scalar.dma_start(out=bt[0:1, :], in_=bfc1.rearrange("(a n) -> a n", a=1))
         ftraw = const.tile([P, C], BF16)
         nc.scalar.dma_start(out=ftraw[:], in_=ft)
+        warm = const.tile([P, 1], F32)
+        nc.vector.memset(warm[:], 1.0)
+        nc.scalar.sqrt(out=warm[:], in_=warm[:])
         ident_f = const.tile([P, P], F32)
         make_identity(nc, ident_f[:])
         ident_b = const.tile([P, P], BF16)
@@ -84,7 +87,9 @@ def tile_joint_module_pa_kernel(tc, fv, ft, W1, b1, g1, be1, m1, v1, Wfc1, bfc1,
             nc.sync.dma_start(out=raw[:], in_=wfc_view[:, 2 * i : 2 * i + 2, :])
             wfraw[i] = raw
 
-        def fv_group(g):
+        tsbs = {}
+
+        def fv_transposes(g):
             words = fvraw[g][:].bitcast(F32).rearrange("b (u p m) -> b u p m", u=2, p=P, m=PIX)
             tsb = stage.tile([P, 2560], F32, tag="tsb", bufs=2, name="tsb%d" % g)
             tw = tsb[:].rearrange("p (m b u) -> p m b u", m=10, b=B, u=2)
@@ -98,7 +103,10 @@ def tile_joint_module_pa_kernel(tc, fv, ft, W1, b1, g1, be1, m1, v1, Wfc1, bfc1,
                     out=tw[:, m0 : m0 + nm, :, :],
                     in_=bank[:, 0:nm, :, :].rearrange("p m u b -> p m b u"),
                 )
-            fb = tsb[:].bitcast(BF16)
+            tsbs[g] = tsb
+
+        def fv_regroup(g):
+            fb = tsbs[g][:].bitcast(BF16)
             gr = stage.tile([P, PIX * 512], BF16, tag="gr", bufs=2, align_bytes=64, name="gr%d" % g)
             grv = gr[:].rearrange("p (q j a) -> p q j a", q=PIX, j=256, a=2)
             even = (
@@ -209,27 +217,35 @@ def tile_joint_module_pa_kernel(tc, fv, ft, W1, b1, g1, be1, m1, v1, Wfc1, bfc1,
 
         CHUNKS = ((0, 512), (512, 512), (1024, 128))
 
-        def conv(ot, s_t, t_t):
-            y = stage.tile([P, COLS], F32, tag="y", bufs=2, name="y%d" % ot)
-            for c0, n in CHUNKS:
+        def mx_pass(acc, ot, g, c0, n):
+            nc.tensor.matmul_mx(
+                out=acc[:],
+                lhsT=w1c[:, ot, g * P : (g + 1) * P].bitcast(FP8X4),
+                lhsT_scale=w1s[:, ot, g * P : (g + 1) * P],
+                rhs=fvc[:, g, c0 : c0 + n].bitcast(FP8X4),
+                rhs_scale=fvs[:, g, c0 : c0 + n],
+                start=(g == 0),
+                stop=(g == GROUPS - 1),
+            )
+
+        def bn_relu(y, acc, ot, c0, n, s_t, t_t):
+            nc.scalar.activation(
+                out=y[:, c0 : c0 + n],
+                in_=acc[:],
+                func=ACT.Relu,
+                bias=t_t[:, ot : ot + 1],
+                scale=s_t[:, ot : ot + 1],
+            )
+
+        def conv(ot, s_t, t_t, chunks, y):
+            for c0, n in chunks:
                 acc = psum.tile([P, n], F32, tag="bank", name="acc")
                 for g in range(GROUPS):
-                    nc.tensor.matmul_mx(
-                        out=acc[:],
-                        lhsT=w1c[:, ot, g * P : (g + 1) * P].bitcast(FP8X4),
-                        lhsT_scale=w1s[:, ot, g * P : (g + 1) * P],
-                        rhs=fvc[:, g, c0 : c0 + n].bitcast(FP8X4),
-                        rhs_scale=fvs[:, g, c0 : c0 + n],
-                        start=(g == 0),
-                        stop=(g == GROUPS - 1),
-                    )
-                nc.scalar.activation(
-                    out=y[:, c0 : c0 + n],
-                    in_=acc[:],
-                    func=ACT.Relu,
-                    bias=t_t[:, ot : ot + 1],
-                    scale=s_t[:, ot : ot + 1],
-                )
+                    mx_pass(acc, ot, g, c0, n)
+                bn_relu(y, acc, ot, c0, n, s_t, t_t)
+
+        def new_y(ot):
+            y = stage.tile([P, COLS], F32, tag="y", bufs=2, name="y%d" % ot)
             return y
 
         def finish(ot, y):
@@ -252,45 +268,60 @@ def tile_joint_module_pa_kernel(tc, fv, ft, W1, b1, g1, be1, m1, v1, Wfc1, bfc1,
                 out=out_flat[:, ot * COLS : (ot + 1) * COLS], in_=osb[:].rearrange("b o x -> b (o x)")
             )
 
-        with tc.manual_schedule():
-            load_fv(0)
-            load_fv(1)
-            load_w(0)
-            load_fv(2)
-            prev = None
-            extra = {0: lambda: load_w(1), 1: lambda: load_wf(0), 2: lambda: load_wf(1)}
-            for g in range(GROUPS):
-                gr = fv_group(g)
+        EARLY = ((0, 0), (0, 512), (1, 0), (1, 512))
+        load_fv(0)
+        load_w(0)
+        load_fv(1)
+        load_w(1)
+        load_fv(2)
+        fv_transposes(0)
+        s_t, t_t = params()
+        wgrs = {0: w_tile(0)}
+        fv_transposes(1)
+        grs = {0: fv_regroup(0)}
+        w_quant(0, wgrs[0])
+        wgrs[1] = w_tile(1)
+        ft_transposes()
+        open_acc = {}
+        extra = {0: lambda: load_w(2), 1: lambda: load_wf(0), 2: lambda: load_wf(1)}
+        for g in range(GROUPS):
+            if g + 3 < GROUPS:
+                load_fv(g + 3)
+                extra[g]()
+            if g + 2 < GROUPS:
+                fv_transposes(g + 2)
+            if g + 1 < GROUPS:
+                grs[g + 1] = fv_regroup(g + 1)
+            fv_quant(g, grs[g])
+            if g == 0:
+                w_quant(1, wgrs[1])
+            for ot, c0 in EARLY:
                 if g == 0:
-                    s_t, t_t = params()
-                    ft_transposes()
-                if g + 3 < GROUPS:
-                    load_fv(g + 3)
-                    extra[g]()
-                if prev is not None:
-                    fv_quant(g - 1, prev)
-                prev = gr
-            wgr0 = w_tile(0)
-            fv_quant(GROUPS - 1, prev)
-            w_quant(0, wgr0)
-            load_w(2)
-            wgr1 = w_tile(1)
-            w_quant(1, wgr1)
-            wfc_half(0)
-            load_wf(2)
-            load_wf(3)
-            gate_half(0)
-            ys = {}
-            for ot in range(OT):
-                ys[ot] = conv(ot, s_t, t_t)
-                if ot + 3 < OT:
-                    load_w(ot + 3)
-                if ot + 2 < OT:
-                    wgr = w_tile(ot + 2)
-                    w_quant(ot + 2, wgr)
-                if ot == 0:
-                    wfc_half(1)
-                    gate_half(1)
-                if ot >= 1:
-                    finish(ot - 1, ys[ot - 1])
-            finish(OT - 1, ys[OT - 1])
+                    acc = psum.tile([P, 512], F32, tag="bank", name="early")
+                    open_acc[(ot, c0)] = acc
+                mx_pass(open_acc[(ot, c0)], ot, g, c0, 512)
+        ys = {}
+        for ot in range(OT):
+            ys[ot] = new_y(ot)
+            if ot < 2:
+                bn_relu(ys[ot], open_acc[(ot, 0)], ot, 0, 512, s_t, t_t)
+                bn_relu(ys[ot], open_acc[(ot, 512)], ot, 512, 512, s_t, t_t)
+                conv(ot, s_t, t_t, CHUNKS[2:], ys[ot])
+            else:
+                conv(ot, s_t, t_t, CHUNKS, ys[ot])
+            if ot + 3 < OT:
+                load_w(ot + 3)
+            if ot + 2 < OT:
+                wgr = w_tile(ot + 2)
+                w_quant(ot + 2, wgr)
+            if ot == 0:
+                wfc_half(0)
+                load_wf(2)
+                load_wf(3)
+                gate_half(0)
+            if ot == 1:
+                wfc_half(1)
+                gate_half(1)
+            if ot >= 1:
+                finish(ot - 1, ys[ot - 1])
+        finish(OT - 1, ys[OT - 1])

@@ -18,6 +18,7 @@ C3 = 3072
 PIX = 9
 GROUPS = 6
 OT = 8
+ROUNDS = ((0, 256), (256, 256), (512, 256), (768, 128), (896, 128))
 COLS = PIX * B
 EPS = 1e-5
 FLOPS = 2 * C * C3 * COLS + 2 * B * C * C
@@ -48,10 +49,10 @@ def tile_joint_module_pa_kernel(tc, fv, ft, W1, b1, g1, be1, m1, v1, Wfc1, bfc1,
         ones = const.tile([P, P], BF16)
         nc.vector.memset(ones[:], 1.0)
         for v, vec in enumerate((b1, g1, be1, m1, v1)):
-            nc.scalar.dma_start(out=ptile[8 * v : 8 * v + 8, :], in_=vec.rearrange("(t p) -> t p", p=P))
+            nc.sync.dma_start(out=ptile[8 * v : 8 * v + 8, :], in_=vec.rearrange("(t p) -> t p", p=P))
         nc.scalar.dma_start(out=bt[0:1, :], in_=bfc1.rearrange("(a n) -> a n", a=1))
         ftraw = const.tile([P, C], BF16)
-        nc.scalar.dma_start(out=ftraw[:], in_=ft)
+        nc.sync.dma_start(out=ftraw[:], in_=ft)
         warm = const.tile([P, 1], F32)
         nc.vector.memset(warm[:], 1.0)
         nc.scalar.sqrt(out=warm[:], in_=warm[:])
@@ -62,18 +63,20 @@ def tile_joint_module_pa_kernel(tc, fv, ft, W1, b1, g1, be1, m1, v1, Wfc1, bfc1,
 
         fvc = keep.tile([P, GROUPS, COLS], U32, align_bytes=64)
         fvs = keep.tile([P, GROUPS, COLS], U8, align_bytes=64)
-        w1c = keep.tile([P, OT, GROUPS * P], U32, align_bytes=64)
-        w1s = keep.tile([P, OT, GROUPS * P], U8, align_bytes=64)
-        wfcT = keep.tile([P, 4 * C], F32)
+        w1c = keep.tile([P, GROUPS * C], U32, align_bytes=64)
+        w1s = keep.tile([P, GROUPS * C], U8, align_bytes=64)
         ftT = keep.tile([P, 4 * B], F32)
         gate = keep.tile([P, C], F32)
+        s_bc = keep.tile([P, C], F32)
+        t_bc = keep.tile([P, C], F32)
 
+        pools = {}
         fvraw = {}
         wraw = {}
         wfraw = {}
 
         def load_fv(g):
-            raw = stage.tile([P, 512 * PIX], BF16, tag="fvraw", bufs=3, name="fvraw%d" % g)
+            raw = pools["front"].tile([P, 512 * PIX], BF16, tag="fvraw", bufs=3, name="fvraw%d" % g)
             nc.sync.dma_start(out=raw[:], in_=fv_flat[:, g * 4608 : (g + 1) * 4608])
             fvraw[g] = raw
 
@@ -91,7 +94,7 @@ def tile_joint_module_pa_kernel(tc, fv, ft, W1, b1, g1, be1, m1, v1, Wfc1, bfc1,
 
         def fv_transposes(g):
             words = fvraw[g][:].bitcast(F32).rearrange("b (u p m) -> b u p m", u=2, p=P, m=PIX)
-            tsb = stage.tile([P, 2560], F32, tag="tsb", bufs=2, name="tsb%d" % g)
+            tsb = pools["front"].tile([P, 2560], F32, tag="tsb", bufs=2, name="tsb%d" % g)
             tw = tsb[:].rearrange("p (m b u) -> p m b u", m=10, b=B, u=2)
             for m0 in range(0, PIX, 2):
                 nm = min(2, PIX - m0)
@@ -107,7 +110,7 @@ def tile_joint_module_pa_kernel(tc, fv, ft, W1, b1, g1, be1, m1, v1, Wfc1, bfc1,
 
         def fv_regroup(g):
             fb = tsbs[g][:].bitcast(BF16)
-            gr = stage.tile([P, PIX * 512], BF16, tag="gr", bufs=2, align_bytes=64, name="gr%d" % g)
+            gr = pools["front"].tile([P, PIX * 512], BF16, tag="gr", bufs=2, align_bytes=64, name="gr%d" % g)
             grv = gr[:].rearrange("p (q j a) -> p q j a", q=PIX, j=256, a=2)
             even = (
                 fb[:, 0:4098]
@@ -156,12 +159,14 @@ def tile_joint_module_pa_kernel(tc, fv, ft, W1, b1, g1, be1, m1, v1, Wfc1, bfc1,
             return wgr
 
         def w_quant(ot, wgr):
-            nc.vector.quantize_mx(
-                out=w1c[:, ot, 0:512].bitcast(FP8X4), scales=w1s[:, ot, 0:512], in_=wgr[:, 0:2048]
-            )
-            nc.vector.quantize_mx(
-                out=w1c[:, ot, 512:768].bitcast(FP8X4), scales=w1s[:, ot, 512:768], in_=wgr[:, 2048:3072]
-            )
+            o0, n = [rd for rd in ROUNDS if rd[0] <= ot * P < rd[0] + rd[1]][0]
+            for g in range(GROUPS):
+                c0 = GROUPS * o0 + g * n + ot * P - o0
+                nc.vector.quantize_mx(
+                    out=w1c[:, c0 : c0 + P].bitcast(FP8X4),
+                    scales=w1s[:, c0 : c0 + P],
+                    in_=wgr[:, g * 512 : (g + 1) * 512],
+                )
 
         def params():
             pbank = psum.tile([P, P], BF16, tag="bank", name="pbank")
@@ -180,6 +185,15 @@ def tile_joint_module_pa_kernel(tc, fv, ft, W1, b1, g1, be1, m1, v1, Wfc1, bfc1,
             nc.vector.tensor_add(out=t_t[:], in0=t_t[:], in1=prm[:, 16:24])
             return s_t, t_t
 
+        def spread(s_t, t_t):
+            for col, wide in ((s_t, s_bc), (t_t, t_bc)):
+                for h in range(2):
+                    bank = psum.tile([P, 4, P], F32, tag="bank", name="bcbank")
+                    for i in range(4):
+                        ot = 4 * h + i
+                        nc.tensor.transpose(bank[:, i, :], col[:, ot : ot + 1].to_broadcast([P, P]), ident_f[:])
+                    nc.scalar.copy(out=wide[:, h * 512 : (h + 1) * 512], in_=bank[:].rearrange("p i o -> p (i o)"))
+
         def ft_transposes():
             words = ftraw[:].bitcast(F32)
             bank = psum.tile([P, 4, B], F32, tag="bank", name="ftbank")
@@ -187,141 +201,142 @@ def tile_joint_module_pa_kernel(tc, fv, ft, W1, b1, g1, be1, m1, v1, Wfc1, bfc1,
                 nc.tensor.transpose(bank[:, kc, :], words[:, kc * P : (kc + 1) * P], ident_f[:])
             nc.scalar.copy(out=ftT[:], in_=bank[:].rearrange("p k b -> p (k b)"))
 
-        def wfc_half(h):
+        def gate_half(h):
+            fvw = ftT[:].bitcast(BF16).rearrange("p (k b e) -> p k b e", k=4, b=B, e=2)
+            wfts = []
             for kc in range(4):
                 bank = psum.tile([P, 4, P], F32, tag="bank", name="wfbank")
                 for i in range(4):
                     ot = 4 * h + i
                     words = wfraw[ot // 2][:, ot % 2, :].bitcast(F32)
                     nc.tensor.transpose(bank[:, i, :], words[:, kc * P : (kc + 1) * P], ident_f[:])
-                nc.scalar.copy(
-                    out=wfcT[:, kc * C + h * 512 : kc * C + (h + 1) * 512],
-                    in_=bank[:].rearrange("p i o -> p (i o)"),
-                )
-
-        def gate_half(h):
-            wv = wfcT[:].bitcast(BF16).rearrange("p (k o e) -> p k o e", k=4, o=C, e=2)
-            fvw = ftT[:].bitcast(BF16).rearrange("p (k b e) -> p k b e", k=4, b=B, e=2)
+                wft = stage.tile([P, 512], F32, tag="wft", bufs=4, name="wft")
+                nc.scalar.copy(out=wft[:], in_=bank[:].rearrange("p i o -> p (i o)"))
+                wfts.append(wft)
             acc = psum.tile([P, 512], F32, tag="bank", name="gbank")
             for kc in range(4):
+                wv = wfts[kc][:].bitcast(BF16).rearrange("p (o e) -> p o e", e=2)
                 for e in range(2):
                     nc.tensor.matmul(
                         acc[:],
                         lhsT=fvw[:, kc, :, e],
-                        rhs=wv[:, kc, h * 512 : (h + 1) * 512, e],
+                        rhs=wv[:, :, e],
                         start=(kc == 0 and e == 0),
                         stop=False,
                     )
             nc.tensor.matmul(acc[:], lhsT=ones[:], rhs=bt[:, h * 512 : (h + 1) * 512], start=False, stop=True)
-            nc.vector.tensor_scalar_add(out=gate[:, h * 512 : (h + 1) * 512], in0=acc[:], scalar1=1.0)
+            nc.scalar.activation(out=gate[:, h * 512 : (h + 1) * 512], in_=acc[:], func=ACT.Copy, bias=1.0, scale=1.0)
 
-        CHUNKS = ((0, 512), (512, 512), (1024, 128))
-
-        def mx_pass(acc, ot, g, c0, n):
+        def mx_pass(acc, o0, n, g, pix):
+            q = slot_of(pix)
+            c0 = GROUPS * o0 + g * n
             nc.tensor.matmul_mx(
-                out=acc[:],
-                lhsT=w1c[:, ot, g * P : (g + 1) * P].bitcast(FP8X4),
-                lhsT_scale=w1s[:, ot, g * P : (g + 1) * P],
-                rhs=fvc[:, g, c0 : c0 + n].bitcast(FP8X4),
-                rhs_scale=fvs[:, g, c0 : c0 + n],
+                out=acc,
+                lhsT=fvc[:, g, q * B : (q + 1) * B].bitcast(FP8X4),
+                lhsT_scale=fvs[:, g, q * B : (q + 1) * B],
+                rhs=w1c[:, c0 : c0 + n].bitcast(FP8X4),
+                rhs_scale=w1s[:, c0 : c0 + n],
                 start=(g == 0),
                 stop=(g == GROUPS - 1),
             )
 
-        def bn_relu(y, acc, ot, c0, n, s_t, t_t):
-            nc.scalar.activation(
-                out=y[:, c0 : c0 + n],
-                in_=acc[:],
-                func=ACT.Relu,
-                bias=t_t[:, ot : ot + 1],
-                scale=s_t[:, ot : ot + 1],
-            )
-
-        def conv(ot, s_t, t_t, chunks, y):
-            for c0, n in chunks:
-                acc = psum.tile([P, n], F32, tag="bank", name="acc")
-                for g in range(GROUPS):
-                    mx_pass(acc, ot, g, c0, n)
-                bn_relu(y, acc, ot, c0, n, s_t, t_t)
-
-        def new_y(ot):
-            y = stage.tile([P, COLS], F32, tag="y", bufs=2, name="y%d" % ot)
-            return y
-
-        def finish(ot, y):
-            planes = stage.tile([P, PIX, P], F32, tag="planes", bufs=2, name="planes%d" % ot)
-            for x0 in range(0, PIX, 4):
-                nx = min(4, PIX - x0)
-                z = psum.tile([P, nx, P], F32, tag="bank", name="z")
-                for i in range(nx):
-                    q = slot_of(x0 + i)
-                    nc.tensor.transpose(z[:, i, :], y[:, q * B : (q + 1) * B], ident_f[:])
-                nc.scalar.copy(out=planes[:, x0 : x0 + nx, :], in_=z[:])
-            osb = stage.tile([P, P, PIX], F32, tag="osb", bufs=3, name="osb%d" % ot)
+        def affine(planes, acc, o0, n, x0, nx, adder):
             nc.vector.tensor_tensor(
-                out=osb[:],
-                in0=planes[:].rearrange("b x o -> b o x"),
-                in1=gate[:, ot * P : (ot + 1) * P].unsqueeze(2).to_broadcast([P, P, PIX]),
+                out=planes[:, x0 : x0 + nx, :],
+                in0=acc,
+                in1=s_bc[:, o0 : o0 + n].unsqueeze(1).to_broadcast([P, nx, n]),
                 op=ALU.mult,
             )
-            nc.sync.dma_start(
-                out=out_flat[:, ot * COLS : (ot + 1) * COLS], in_=osb[:].rearrange("b o x -> b (o x)")
+            adder.tensor_tensor(
+                out=planes[:, x0 : x0 + nx, :],
+                in0=planes[:, x0 : x0 + nx, :],
+                in1=t_bc[:, o0 : o0 + n].unsqueeze(1).to_broadcast([P, nx, n]),
+                op=ALU.add,
             )
 
-        EARLY = ((0, 0), (0, 512), (1, 0), (1, 512))
-        load_fv(0)
-        load_w(0)
-        load_fv(1)
-        load_w(1)
-        load_fv(2)
-        fv_transposes(0)
-        s_t, t_t = params()
-        wgrs = {0: w_tile(0)}
-        fv_transposes(1)
-        grs = {0: fv_regroup(0)}
-        w_quant(0, wgrs[0])
-        wgrs[1] = w_tile(1)
-        ft_transposes()
-        open_acc = {}
-        extra = {0: lambda: load_w(2), 1: lambda: load_wf(0), 2: lambda: load_wf(1)}
-        for g in range(GROUPS):
-            if g + 3 < GROUPS:
-                load_fv(g + 3)
-                extra[g]()
-            if g + 2 < GROUPS:
-                fv_transposes(g + 2)
-            if g + 1 < GROUPS:
-                grs[g + 1] = fv_regroup(g + 1)
-            fv_quant(g, grs[g])
-            if g == 0:
-                w_quant(1, wgrs[1])
-            for ot, c0 in EARLY:
+        def finish(planes, o0, n, step):
+            for i0 in range(0, n, step):
+                osb = pools["back"].tile([P, step, PIX], F32, tag="osb", bufs=5, name="osb")
+                nc.vector.scalar_tensor_tensor(
+                    out=osb[:],
+                    in0=planes[:, :, i0 : i0 + step].rearrange("b x o -> b o x"),
+                    scalar=0.0,
+                    in1=gate[:, o0 + i0 : o0 + i0 + step].unsqueeze(2).to_broadcast([P, step, PIX]),
+                    op0=ALU.max,
+                    op1=ALU.mult,
+                )
+                nc.sync.dma_start(
+                    out=out_flat[:, (o0 + i0) * PIX : (o0 + i0 + step) * PIX],
+                    in_=osb[:].rearrange("b o x -> b (o x)"),
+                )
+
+        EARLY = 4
+        with tc.tile_pool(name="front", bufs=2) as front:
+            pools["front"] = front
+            load_w(0)
+            load_fv(0)
+            load_w(1)
+            load_fv(1)
+            load_fv(2)
+            s_t, t_t = params()
+            ft_transposes()
+            wgrs = {0: w_tile(0)}
+            spread(s_t, t_t)
+            fv_transposes(0)
+            w_quant(0, wgrs[0])
+            wgrs[1] = w_tile(1)
+            fv_transposes(1)
+            grs = {0: fv_regroup(0)}
+            open_acc = {}
+            extra = {0: lambda: load_w(2), 1: lambda: load_wf(0), 2: lambda: load_wf(1)}
+            for g in range(GROUPS):
+                if g + 3 < GROUPS:
+                    load_fv(g + 3)
+                    extra[g]()
+                if g + 2 < GROUPS:
+                    fv_transposes(g + 2)
+                if g + 1 < GROUPS:
+                    grs[g + 1] = fv_regroup(g + 1)
+                fv_quant(g, grs[g])
                 if g == 0:
-                    acc = psum.tile([P, 512], F32, tag="bank", name="early")
-                    open_acc[(ot, c0)] = acc
-                mx_pass(open_acc[(ot, c0)], ot, g, c0, 512)
-        ys = {}
-        for ot in range(OT):
-            ys[ot] = new_y(ot)
-            if ot < 2:
-                bn_relu(ys[ot], open_acc[(ot, 0)], ot, 0, 512, s_t, t_t)
-                bn_relu(ys[ot], open_acc[(ot, 512)], ot, 512, 512, s_t, t_t)
-                conv(ot, s_t, t_t, CHUNKS[2:], ys[ot])
-            else:
-                conv(ot, s_t, t_t, CHUNKS, ys[ot])
-            if ot + 3 < OT:
-                load_w(ot + 3)
-            if ot + 2 < OT:
-                wgr = w_tile(ot + 2)
-                w_quant(ot + 2, wgr)
-            if ot == 0:
-                wfc_half(0)
-                load_wf(2)
-                load_wf(3)
-                gate_half(0)
-            if ot == 1:
-                wfc_half(1)
-                gate_half(1)
-            if ot >= 1:
-                finish(ot - 1, ys[ot - 1])
-        finish(OT - 1, ys[OT - 1])
+                    w_quant(1, wgrs[1])
+                for pix in range(EARLY):
+                    if g == 0:
+                        acc = psum.tile([P, 1, 256], F32, tag="bank", name="early")
+                        open_acc[pix] = acc
+                    mx_pass(open_acc[pix][:, 0, :], 0, 256, g, pix)
+                if g == 3:
+                    gate_half(0)
+                    load_wf(2)
+                    load_wf(3)
+                if g == 5:
+                    gate_half(1)
+        pools["back"] = ctx.enter_context(tc.tile_pool(name="back", bufs=2))
+        next_w = 2
+        pending = None
+        for r, (o0, n) in enumerate(ROUNDS):
+            final = r == len(ROUNDS) - 1
+            planes = pools["back"].tile([P, PIX, n], F32, tag="planes", bufs=3, name="planes%d" % r)
+            first = 0
+            if r == 0:
+                for pix in range(EARLY):
+                    affine(planes, open_acc[pix][:], o0, n, pix, 1, nc.gpsimd)
+                first = EARLY
+            per_bank = 512 // n
+            for x0 in range(first, PIX, per_bank):
+                nx = min(per_bank, PIX - x0)
+                acc = psum.tile([P, nx, n], F32, tag="bank", name="acc")
+                for j in range(nx):
+                    for g in range(GROUPS):
+                        mx_pass(acc[:, j, :], o0, n, g, x0 + j)
+                affine(planes, acc[:], o0, n, x0, nx, nc.vector if (final and x0 == 8) else nc.gpsimd)
+                if x0 == first and pending is not None:
+                    finish(*pending)
+                if x0 in (4, 6) and next_w < OT and next_w * P < o0 + n + 256:
+                    if next_w + 1 < OT:
+                        load_w(next_w + 1)
+                    wgr = w_tile(next_w)
+                    w_quant(next_w, wgr)
+                    next_w += 1
+            pending = (planes, o0, n, 64 if final else P)
+        finish(*pending)

@@ -18,7 +18,8 @@ C3 = 3072
 PIX = 9
 GROUPS = 6
 OT = 8
-ROUNDS = ((0, 256), (256, 256), (512, 256), (768, 128), (896, 128))
+ROUNDS = ((0, 256), (256, 256), (512, 256), (768, 128))
+LAST = (896, 128)
 COLS = PIX * B
 EPS = 1e-5
 FLOPS = 2 * C * C3 * COLS + 2 * B * C * C
@@ -159,7 +160,7 @@ def tile_joint_module_pa_kernel(tc, fv, ft, W1, b1, g1, be1, m1, v1, Wfc1, bfc1,
             return wgr
 
         def w_quant(ot, wgr):
-            o0, n = [rd for rd in ROUNDS if rd[0] <= ot * P < rd[0] + rd[1]][0]
+            o0, n = [rd for rd in ROUNDS + (LAST,) if rd[0] <= ot * P < rd[0] + rd[1]][0]
             for g in range(GROUPS):
                 c0 = GROUPS * o0 + g * n + ot * P - o0
                 nc.vector.quantize_mx(
@@ -270,6 +271,50 @@ def tile_joint_module_pa_kernel(tc, fv, ft, W1, b1, g1, be1, m1, v1, Wfc1, bfc1,
                     in_=osb[:].rearrange("b o x -> b (o x)"),
                 )
 
+        def last_tile(s_t, t_t):
+            o0, n = LAST
+            ot = o0 // P
+            y = pools["back"].tile([P, COLS], F32, tag="y", bufs=1, name="y")
+            planes = pools["back"].tile([P, PIX, n], F32, tag="planes", bufs=3, name="planes_last")
+            for c0, w in ((0, 512), (512, 512), (1024, 128)):
+                acc = psum.tile([P, w], F32, tag="bank", name="acc_last")
+                for g in range(GROUPS):
+                    k0 = GROUPS * o0 + g * n
+                    nc.tensor.matmul_mx(
+                        out=acc[:],
+                        lhsT=w1c[:, k0 : k0 + n].bitcast(FP8X4),
+                        lhsT_scale=w1s[:, k0 : k0 + n],
+                        rhs=fvc[:, g, c0 : c0 + w].bitcast(FP8X4),
+                        rhs_scale=fvs[:, g, c0 : c0 + w],
+                        start=(g == 0),
+                        stop=(g == GROUPS - 1),
+                    )
+                nc.scalar.activation(
+                    out=y[:, c0 : c0 + w],
+                    in_=acc[:],
+                    func=ACT.Relu,
+                    bias=t_t[:, ot : ot + 1],
+                    scale=s_t[:, ot : ot + 1],
+                )
+            pairs = planes[:, 0:8, :].rearrange("b (i two) o -> b two i o", two=2)
+            for q0, nq, view in ((0, 4, pairs[:, 0, :, :]), (4, 4, pairs[:, 1, :, :]), (8, 1, planes[:, 8:9, :])):
+                z = psum.tile([P, nq, P], F32, tag="bank", name="z")
+                for i in range(nq):
+                    nc.tensor.transpose(z[:, i, :], y[:, (q0 + i) * B : (q0 + i + 1) * B], ident_f[:])
+                nc.scalar.copy(out=view, in_=z[:])
+            for i0 in range(0, n, 64):
+                osb = pools["back"].tile([P, 64, PIX], F32, tag="osb", bufs=5, name="osb_last")
+                nc.vector.tensor_tensor(
+                    out=osb[:],
+                    in0=planes[:, :, i0 : i0 + 64].rearrange("b x o -> b o x"),
+                    in1=gate[:, o0 + i0 : o0 + i0 + 64].unsqueeze(2).to_broadcast([P, 64, PIX]),
+                    op=ALU.mult,
+                )
+                nc.sync.dma_start(
+                    out=out_flat[:, (o0 + i0) * PIX : (o0 + i0 + 64) * PIX],
+                    in_=osb[:].rearrange("b o x -> b (o x)"),
+                )
+
         EARLY = 4
         with tc.tile_pool(name="front", bufs=2) as front:
             pools["front"] = front
@@ -315,12 +360,11 @@ def tile_joint_module_pa_kernel(tc, fv, ft, W1, b1, g1, be1, m1, v1, Wfc1, bfc1,
         next_w = 2
         pending = None
         for r, (o0, n) in enumerate(ROUNDS):
-            final = r == len(ROUNDS) - 1
             planes = pools["back"].tile([P, PIX, n], F32, tag="planes", bufs=3, name="planes%d" % r)
             first = 0
             if r == 0:
                 for pix in range(EARLY):
-                    affine(planes, open_acc[pix][:], o0, n, pix, 1, nc.gpsimd)
+                    affine(planes, open_acc[pix][:], o0, n, pix, 1, nc.vector)
                 first = EARLY
             per_bank = 512 // n
             for x0 in range(first, PIX, per_bank):
@@ -329,7 +373,7 @@ def tile_joint_module_pa_kernel(tc, fv, ft, W1, b1, g1, be1, m1, v1, Wfc1, bfc1,
                 for j in range(nx):
                     for g in range(GROUPS):
                         mx_pass(acc[:, j, :], o0, n, g, x0 + j)
-                affine(planes, acc[:], o0, n, x0, nx, nc.vector if (final and x0 == 8) else nc.gpsimd)
+                affine(planes, acc[:], o0, n, x0, nx, nc.vector)
                 if x0 == first and pending is not None:
                     finish(*pending)
                 if x0 in (4, 6) and next_w < OT and next_w * P < o0 + n + 256:
@@ -338,5 +382,6 @@ def tile_joint_module_pa_kernel(tc, fv, ft, W1, b1, g1, be1, m1, v1, Wfc1, bfc1,
                     wgr = w_tile(next_w)
                     w_quant(next_w, wgr)
                     next_w += 1
-            pending = (planes, o0, n, 64 if final else P)
+            pending = (planes, o0, n, P)
         finish(*pending)
+        last_tile(s_t, t_t)

@@ -18,17 +18,10 @@ C3 = 3072
 PIX = 9
 GROUPS = 6
 OT = 8
-ROUNDS = ((0, 256), (256, 256), (512, 256), (768, 128))
-LAST = (896, 128)
 COLS = PIX * B
 EPS = 1e-5
+PATH = ("tensor", "tensor", "vector", "tensor", "vector", "tensor", "vector", "tensor")
 FLOPS = 2 * C * C3 * COLS + 2 * B * C * C
-
-
-def slot_of(pix):
-    if pix == 8:
-        return 8
-    return (pix % 2) * 4 + pix // 2
 
 
 def tile_joint_module_pa_kernel(tc, fv, ft, W1, b1, g1, be1, m1, v1, Wfc1, bfc1, out):
@@ -49,7 +42,7 @@ def tile_joint_module_pa_kernel(tc, fv, ft, W1, b1, g1, be1, m1, v1, Wfc1, bfc1,
         nc.vector.memset(bt[:], 0.0)
         ones = const.tile([P, P], BF16)
         nc.vector.memset(ones[:], 1.0)
-        for v, vec in enumerate((b1, g1, be1, m1, v1)):
+        for v, vec in enumerate((b1, g1, be1, m1, v1, bfc1)):
             nc.sync.dma_start(out=ptile[8 * v : 8 * v + 8, :], in_=vec.rearrange("(t p) -> t p", p=P))
         nc.scalar.dma_start(out=bt[0:1, :], in_=bfc1.rearrange("(a n) -> a n", a=1))
         ftraw = const.tile([P, C], BF16)
@@ -64,12 +57,11 @@ def tile_joint_module_pa_kernel(tc, fv, ft, W1, b1, g1, be1, m1, v1, Wfc1, bfc1,
 
         fvc = keep.tile([P, GROUPS, COLS], U32, align_bytes=64)
         fvs = keep.tile([P, GROUPS, COLS], U8, align_bytes=64)
-        w1c = keep.tile([P, GROUPS * C], U32, align_bytes=64)
-        w1s = keep.tile([P, GROUPS * C], U8, align_bytes=64)
+        w1c = keep.tile([P, OT, GROUPS * P], U32, align_bytes=64)
+        w1s = keep.tile([P, OT, GROUPS * P], U8, align_bytes=64)
         ftT = keep.tile([P, 4 * B], F32)
-        gate = keep.tile([P, C], F32)
-        s_bc = keep.tile([P, C], F32)
-        t_bc = keep.tile([P, C], F32)
+        gate = keep.tile([P, C], F32, align_bytes=64)
+        bp1 = keep.tile([P, OT], F32)
 
         pools = {}
         fvraw = {}
@@ -131,8 +123,9 @@ def tile_joint_module_pa_kernel(tc, fv, ft, W1, b1, g1, be1, m1, v1, Wfc1, bfc1,
                 .rearrange("p a (j h) -> p a j h", j=256, h=2)[:, :, :, 0]
                 .rearrange("p a j -> p j a")
             )
-            nc.vector.tensor_copy(out=grv[:, 0:4, :, :], in_=even)
-            nc.vector.tensor_copy(out=grv[:, 4:8, :, :], in_=odd)
+            pairs = grv[:, 0:8, :, :].rearrange("p (n two) j a -> p two n j a", two=2)
+            nc.vector.tensor_copy(out=pairs[:, 0, :, :, :], in_=even)
+            nc.vector.tensor_copy(out=pairs[:, 1, :, :, :], in_=odd)
             nc.vector.tensor_copy(out=grv[:, 8, :, :], in_=last)
             return gr
 
@@ -160,20 +153,19 @@ def tile_joint_module_pa_kernel(tc, fv, ft, W1, b1, g1, be1, m1, v1, Wfc1, bfc1,
             return wgr
 
         def w_quant(ot, wgr):
-            o0, n = [rd for rd in ROUNDS + (LAST,) if rd[0] <= ot * P < rd[0] + rd[1]][0]
-            for g in range(GROUPS):
-                c0 = GROUPS * o0 + g * n + ot * P - o0
-                nc.vector.quantize_mx(
-                    out=w1c[:, c0 : c0 + P].bitcast(FP8X4),
-                    scales=w1s[:, c0 : c0 + P],
-                    in_=wgr[:, g * 512 : (g + 1) * 512],
-                )
+            nc.vector.quantize_mx(
+                out=w1c[:, ot, 0:512].bitcast(FP8X4), scales=w1s[:, ot, 0:512], in_=wgr[:, 0:2048]
+            )
+            nc.vector.quantize_mx(
+                out=w1c[:, ot, 512:768].bitcast(FP8X4), scales=w1s[:, ot, 512:768], in_=wgr[:, 2048:3072]
+            )
 
         def params():
             pbank = psum.tile([P, P], BF16, tag="bank", name="pbank")
             nc.tensor.transpose(pbank[:], ptile[:], ident_b[:])
-            prm = const.tile([P, 40], F32)
-            nc.vector.tensor_copy(out=prm[:], in_=pbank[:, 0:40])
+            prm = const.tile([P, 48], F32)
+            nc.vector.tensor_copy(out=prm[:], in_=pbank[:, 0:48])
+            nc.vector.tensor_scalar_add(out=bp1[:], in0=prm[:, 40:48], scalar1=1.0)
             s_t = const.tile([P, OT], F32)
             t_t = const.tile([P, OT], F32)
             tmp = const.tile([P, OT], F32)
@@ -186,15 +178,6 @@ def tile_joint_module_pa_kernel(tc, fv, ft, W1, b1, g1, be1, m1, v1, Wfc1, bfc1,
             nc.vector.tensor_add(out=t_t[:], in0=t_t[:], in1=prm[:, 16:24])
             return s_t, t_t
 
-        def spread(s_t, t_t):
-            for col, wide in ((s_t, s_bc), (t_t, t_bc)):
-                for h in range(2):
-                    bank = psum.tile([P, 4, P], F32, tag="bank", name="bcbank")
-                    for i in range(4):
-                        ot = 4 * h + i
-                        nc.tensor.transpose(bank[:, i, :], col[:, ot : ot + 1].to_broadcast([P, P]), ident_f[:])
-                    nc.scalar.copy(out=wide[:, h * 512 : (h + 1) * 512], in_=bank[:].rearrange("p i o -> p (i o)"))
-
         def ft_transposes():
             words = ftraw[:].bitcast(F32)
             bank = psum.tile([P, 4, B], F32, tag="bank", name="ftbank")
@@ -202,120 +185,119 @@ def tile_joint_module_pa_kernel(tc, fv, ft, W1, b1, g1, be1, m1, v1, Wfc1, bfc1,
                 nc.tensor.transpose(bank[:, kc, :], words[:, kc * P : (kc + 1) * P], ident_f[:])
             nc.scalar.copy(out=ftT[:], in_=bank[:].rearrange("p k b -> p (k b)"))
 
-        def gate_half(h):
+        wfts = {}
+
+        def gate_transposes(ot):
+            bank = psum.tile([P, 4, P], F32, tag="bank", name="wfbank")
+            words = wfraw[ot // 2][:, ot % 2, :].bitcast(F32)
+            for kc in range(4):
+                nc.tensor.transpose(bank[:, kc, :], words[:, kc * P : (kc + 1) * P], ident_f[:])
+            wft = stage.tile([P, 4 * P], F32, tag="wft", bufs=4, name="wft")
+            nc.scalar.copy(out=wft[:], in_=bank[:].rearrange("p k o -> p (k o)"))
+            wfts[ot] = wft
+
+        def gate_tile(ot):
+            wv = wfts[ot][:].bitcast(BF16).rearrange("p (k o e) -> p k o e", k=4, o=P, e=2)
             fvw = ftT[:].bitcast(BF16).rearrange("p (k b e) -> p k b e", k=4, b=B, e=2)
-            wfts = []
+            cols = slice(ot * P, (ot + 1) * P)
+            acc = psum.tile([P, P], F32, tag="bank", name="gbank")
+            on_vector = PATH[ot] == "vector"
             for kc in range(4):
-                bank = psum.tile([P, 4, P], F32, tag="bank", name="wfbank")
-                for i in range(4):
-                    ot = 4 * h + i
-                    words = wfraw[ot // 2][:, ot % 2, :].bitcast(F32)
-                    nc.tensor.transpose(bank[:, i, :], words[:, kc * P : (kc + 1) * P], ident_f[:])
-                wft = stage.tile([P, 512], F32, tag="wft", bufs=4, name="wft")
-                nc.scalar.copy(out=wft[:], in_=bank[:].rearrange("p i o -> p (i o)"))
-                wfts.append(wft)
-            acc = psum.tile([P, 512], F32, tag="bank", name="gbank")
-            for kc in range(4):
-                wv = wfts[kc][:].bitcast(BF16).rearrange("p (o e) -> p o e", e=2)
                 for e in range(2):
                     nc.tensor.matmul(
                         acc[:],
-                        lhsT=fvw[:, kc, :, e],
-                        rhs=wv[:, :, e],
+                        lhsT=(wv if on_vector else fvw)[:, kc, :, e],
+                        rhs=(fvw if on_vector else wv)[:, kc, :, e],
                         start=(kc == 0 and e == 0),
-                        stop=False,
+                        stop=(on_vector and kc == 3 and e == 1),
                     )
-            nc.tensor.matmul(acc[:], lhsT=ones[:], rhs=bt[:, h * 512 : (h + 1) * 512], start=False, stop=True)
-            nc.scalar.activation(out=gate[:, h * 512 : (h + 1) * 512], in_=acc[:], func=ACT.Copy, bias=1.0, scale=1.0)
+            if on_vector:
+                gt = stage.tile([P, B], F32, tag="gt", bufs=2, align_bytes=64, name="gt")
+                nc.scalar.activation(out=gt[:], in_=acc[:], func=ACT.Identity, bias=bp1[:, ot : ot + 1], scale=1.0)
+                nc.vector.transpose(out=gate[:, cols], in_=gt[:])
+            else:
+                nc.tensor.matmul(acc[:], lhsT=ones[:], rhs=bt[:, cols], start=False, stop=True)
+                nc.scalar.activation(out=gate[:, cols], in_=acc[:], func=ACT.Copy, bias=1.0, scale=1.0)
 
-        def mx_pass(acc, o0, n, g, pix):
-            q = slot_of(pix)
-            c0 = GROUPS * o0 + g * n
+        CHUNKS = ((0, 512), (512, 512), (1024, 128))
+
+        def mx_pass(acc, ot, g, c0, n):
             nc.tensor.matmul_mx(
-                out=acc,
-                lhsT=fvc[:, g, q * B : (q + 1) * B].bitcast(FP8X4),
-                lhsT_scale=fvs[:, g, q * B : (q + 1) * B],
-                rhs=w1c[:, c0 : c0 + n].bitcast(FP8X4),
-                rhs_scale=w1s[:, c0 : c0 + n],
+                out=acc[:],
+                lhsT=w1c[:, ot, g * P : (g + 1) * P].bitcast(FP8X4),
+                lhsT_scale=w1s[:, ot, g * P : (g + 1) * P],
+                rhs=fvc[:, g, c0 : c0 + n].bitcast(FP8X4),
+                rhs_scale=fvs[:, g, c0 : c0 + n],
                 start=(g == 0),
                 stop=(g == GROUPS - 1),
             )
 
-        def affine(planes, acc, o0, n, x0, nx, adder):
+        def bn_relu(y, acc, ot, c0, n, s_t, t_t):
+            nc.scalar.activation(
+                out=y[:, c0 : c0 + n],
+                in_=acc[:],
+                func=ACT.Relu,
+                bias=t_t[:, ot : ot + 1],
+                scale=s_t[:, ot : ot + 1],
+            )
+
+        def conv(ot, s_t, t_t, chunks, y):
+            for c0, n in chunks:
+                acc = psum.tile([P, n], F32, tag="bank", name="acc")
+                for g in range(GROUPS):
+                    mx_pass(acc, ot, g, c0, n)
+                bn_relu(y, acc, ot, c0, n, s_t, t_t)
+
+        def new_y(ot):
+            y = pools["back"].tile([P, COLS], F32, tag="y", bufs=3, align_bytes=64, name="y%d" % ot)
+            return y
+
+        def finish_on_vector(ot, y):
+            yt = pools["back"].tile([P, COLS], F32, tag="yt", bufs=2, align_bytes=64, name="yt%d" % ot)
+            nc.vector.transpose(out=yt[:, 0:1024], in_=y[:, 0:1024])
+            nc.vector.transpose(out=yt[:, 1024:1152], in_=y[:, 1024:1152])
+            osb = pools["back"].tile([P, P, PIX], F32, tag="osb", bufs=4, name="osbv%d" % ot)
             nc.vector.tensor_tensor(
-                out=planes[:, x0 : x0 + nx, :],
-                in0=acc,
-                in1=s_bc[:, o0 : o0 + n].unsqueeze(1).to_broadcast([P, nx, n]),
+                out=osb[:],
+                in0=yt[:].rearrange("p (x c) -> p c x", x=PIX),
+                in1=gate[:, ot * P : (ot + 1) * P].unsqueeze(2).to_broadcast([P, P, PIX]),
                 op=ALU.mult,
             )
-            adder.tensor_tensor(
-                out=planes[:, x0 : x0 + nx, :],
-                in0=planes[:, x0 : x0 + nx, :],
-                in1=t_bc[:, o0 : o0 + n].unsqueeze(1).to_broadcast([P, nx, n]),
-                op=ALU.add,
-            )
-
-        def finish(planes, o0, n, step):
-            for i0 in range(0, n, step):
-                osb = pools["back"].tile([P, step, PIX], F32, tag="osb", bufs=5, name="osb")
-                nc.vector.scalar_tensor_tensor(
-                    out=osb[:],
-                    in0=planes[:, :, i0 : i0 + step].rearrange("b x o -> b o x"),
-                    scalar=0.0,
-                    in1=gate[:, o0 + i0 : o0 + i0 + step].unsqueeze(2).to_broadcast([P, step, PIX]),
-                    op0=ALU.max,
-                    op1=ALU.mult,
-                )
+            rows = out_flat.rearrange("(j l) f -> l j f", l=32)
+            for i in range(4):
+                f0 = (ot * P + 32 * i) * PIX
                 nc.sync.dma_start(
-                    out=out_flat[:, (o0 + i0) * PIX : (o0 + i0 + step) * PIX],
-                    in_=osb[:].rearrange("b o x -> b (o x)"),
+                    out=rows[:, :, f0 : f0 + 32 * PIX],
+                    in_=osb[32 * i : 32 * i + 32, :, :].rearrange("l (j o) x -> l j (o x)", j=4),
                 )
 
-        def last_tile(s_t, t_t):
-            o0, n = LAST
-            ot = o0 // P
-            y = pools["back"].tile([P, COLS], F32, tag="y", bufs=1, name="y")
-            planes = pools["back"].tile([P, PIX, n], F32, tag="planes", bufs=3, name="planes_last")
-            for c0, w in ((0, 512), (512, 512), (1024, 128)):
-                acc = psum.tile([P, w], F32, tag="bank", name="acc_last")
-                for g in range(GROUPS):
-                    k0 = GROUPS * o0 + g * n
-                    nc.tensor.matmul_mx(
-                        out=acc[:],
-                        lhsT=w1c[:, k0 : k0 + n].bitcast(FP8X4),
-                        lhsT_scale=w1s[:, k0 : k0 + n],
-                        rhs=fvc[:, g, c0 : c0 + w].bitcast(FP8X4),
-                        rhs_scale=fvs[:, g, c0 : c0 + w],
-                        start=(g == 0),
-                        stop=(g == GROUPS - 1),
-                    )
-                nc.scalar.activation(
-                    out=y[:, c0 : c0 + w],
-                    in_=acc[:],
-                    func=ACT.Relu,
-                    bias=t_t[:, ot : ot + 1],
-                    scale=s_t[:, ot : ot + 1],
-                )
-            pairs = planes[:, 0:8, :].rearrange("b (i two) o -> b two i o", two=2)
-            for q0, nq, view in ((0, 4, pairs[:, 0, :, :]), (4, 4, pairs[:, 1, :, :]), (8, 1, planes[:, 8:9, :])):
-                z = psum.tile([P, nq, P], F32, tag="bank", name="z")
-                for i in range(nq):
-                    nc.tensor.transpose(z[:, i, :], y[:, (q0 + i) * B : (q0 + i + 1) * B], ident_f[:])
-                nc.scalar.copy(out=view, in_=z[:])
-            for i0 in range(0, n, 64):
-                osb = pools["back"].tile([P, 64, PIX], F32, tag="osb", bufs=5, name="osb_last")
+        def finish(ot, y):
+            if PATH[ot] == "vector":
+                finish_on_vector(ot, y)
+                return
+            planes = pools["back"].tile([P, PIX, P], F32, tag="planes", bufs=3, name="planes%d" % ot)
+            for x0 in range(0, PIX, 4):
+                nx = min(4, PIX - x0)
+                z = psum.tile([P, nx, P], F32, tag="bank", name="z")
+                for i in range(nx):
+                    q = x0 + i
+                    nc.tensor.transpose(z[:, i, :], y[:, q * B : (q + 1) * B], ident_f[:])
+                nc.scalar.copy(out=planes[:, x0 : x0 + nx, :], in_=z[:])
+            step = 64 if ot == OT - 1 else P
+            for i0 in range(0, P, step):
+                osb = pools["back"].tile([P, step, PIX], F32, tag="osb", bufs=4, name="osb%d" % ot)
+                o0 = ot * P + i0
                 nc.vector.tensor_tensor(
                     out=osb[:],
-                    in0=planes[:, :, i0 : i0 + 64].rearrange("b x o -> b o x"),
-                    in1=gate[:, o0 + i0 : o0 + i0 + 64].unsqueeze(2).to_broadcast([P, 64, PIX]),
+                    in0=planes[:, :, i0 : i0 + step].rearrange("b x o -> b o x"),
+                    in1=gate[:, o0 : o0 + step].unsqueeze(2).to_broadcast([P, step, PIX]),
                     op=ALU.mult,
                 )
                 nc.sync.dma_start(
-                    out=out_flat[:, (o0 + i0) * PIX : (o0 + i0 + 64) * PIX],
-                    in_=osb[:].rearrange("b o x -> b (o x)"),
+                    out=out_flat[:, o0 * PIX : (o0 + step) * PIX], in_=osb[:].rearrange("b o x -> b (o x)")
                 )
 
-        EARLY = 4
+        EARLY = ((0, 0), (0, 512), (1, 0), (1, 512))
         with tc.tile_pool(name="front", bufs=2) as front:
             pools["front"] = front
             load_w(0)
@@ -326,7 +308,6 @@ def tile_joint_module_pa_kernel(tc, fv, ft, W1, b1, g1, be1, m1, v1, Wfc1, bfc1,
             s_t, t_t = params()
             ft_transposes()
             wgrs = {0: w_tile(0)}
-            spread(s_t, t_t)
             fv_transposes(0)
             w_quant(0, wgrs[0])
             wgrs[1] = w_tile(1)
@@ -345,43 +326,38 @@ def tile_joint_module_pa_kernel(tc, fv, ft, W1, b1, g1, be1, m1, v1, Wfc1, bfc1,
                 fv_quant(g, grs[g])
                 if g == 0:
                     w_quant(1, wgrs[1])
-                for pix in range(EARLY):
+                for ot, c0 in EARLY:
                     if g == 0:
-                        acc = psum.tile([P, 1, 256], F32, tag="bank", name="early")
-                        open_acc[pix] = acc
-                    mx_pass(open_acc[pix][:, 0, :], 0, 256, g, pix)
+                        acc = psum.tile([P, 512], F32, tag="bank", name="early")
+                        open_acc[(ot, c0)] = acc
+                    mx_pass(open_acc[(ot, c0)], ot, g, c0, 512)
                 if g == 3:
-                    gate_half(0)
+                    for ot in range(4):
+                        gate_transposes(ot)
                     load_wf(2)
                     load_wf(3)
+                    for ot in range(4):
+                        gate_tile(ot)
                 if g == 5:
-                    gate_half(1)
+                    for ot in range(4, OT):
+                        gate_transposes(ot)
+                    for ot in range(4, OT):
+                        gate_tile(ot)
         pools["back"] = ctx.enter_context(tc.tile_pool(name="back", bufs=2))
-        next_w = 2
-        pending = None
-        for r, (o0, n) in enumerate(ROUNDS):
-            planes = pools["back"].tile([P, PIX, n], F32, tag="planes", bufs=3, name="planes%d" % r)
-            first = 0
-            if r == 0:
-                for pix in range(EARLY):
-                    affine(planes, open_acc[pix][:], o0, n, pix, 1, nc.vector)
-                first = EARLY
-            per_bank = 512 // n
-            for x0 in range(first, PIX, per_bank):
-                nx = min(per_bank, PIX - x0)
-                acc = psum.tile([P, nx, n], F32, tag="bank", name="acc")
-                for j in range(nx):
-                    for g in range(GROUPS):
-                        mx_pass(acc[:, j, :], o0, n, g, x0 + j)
-                affine(planes, acc[:], o0, n, x0, nx, nc.vector)
-                if x0 == first and pending is not None:
-                    finish(*pending)
-                if x0 in (4, 6) and next_w < OT and next_w * P < o0 + n + 256:
-                    if next_w + 1 < OT:
-                        load_w(next_w + 1)
-                    wgr = w_tile(next_w)
-                    w_quant(next_w, wgr)
-                    next_w += 1
-            pending = (planes, o0, n, P)
-        finish(*pending)
-        last_tile(s_t, t_t)
+        ys = {}
+        for ot in range(OT):
+            ys[ot] = new_y(ot)
+            if ot < 2:
+                bn_relu(ys[ot], open_acc[(ot, 0)], ot, 0, 512, s_t, t_t)
+                bn_relu(ys[ot], open_acc[(ot, 512)], ot, 512, 512, s_t, t_t)
+                conv(ot, s_t, t_t, CHUNKS[2:], ys[ot])
+            else:
+                conv(ot, s_t, t_t, CHUNKS, ys[ot])
+            if ot + 3 < OT:
+                load_w(ot + 3)
+            if ot + 2 < OT:
+                wgr = w_tile(ot + 2)
+                w_quant(ot + 2, wgr)
+            if ot >= 1:
+                finish(ot - 1, ys[ot - 1])
+        finish(OT - 1, ys[OT - 1])

@@ -331,18 +331,6 @@ def tile_joint_module_pa_kernel(tc, fv, ft, W1, b1, g1, be1, m1, v1, Wfc1, bfc1,
                         acc = psum.tile([P, 512], F32, tag="bank", name="early")
                         open_acc[(ot, c0)] = acc
                     mx_pass(open_acc[(ot, c0)], ot, g, c0, 512)
-                if g == 3:
-                    for ot in range(4):
-                        gate_transposes(ot)
-                    load_wf(2)
-                    load_wf(3)
-                    for ot in range(4):
-                        gate_tile(ot)
-                if g == 5:
-                    for ot in range(4, OT):
-                        gate_transposes(ot)
-                    for ot in range(4, OT):
-                        gate_tile(ot)
         pools["back"] = ctx.enter_context(tc.tile_pool(name="back", bufs=2))
         ys = {}
         for ot in range(OT):
@@ -358,6 +346,16 @@ def tile_joint_module_pa_kernel(tc, fv, ft, W1, b1, g1, be1, m1, v1, Wfc1, bfc1,
             if ot + 2 < OT:
                 wgr = w_tile(ot + 2)
                 w_quant(ot + 2, wgr)
-            if ot >= 1:
+            if ot in (2, 3):
+                for i in range(4 * ot - 8, 4 * ot - 4):
+                    gate_transposes(i)
+                if ot == 2:
+                    load_wf(2)
+                    load_wf(3)
+                for i in range(4 * ot - 8, 4 * ot - 4):
+                    gate_tile(i)
+            if ot == 2:
+                finish(0, ys[0])
+            if ot >= 2:
                 finish(ot - 1, ys[ot - 1])
         finish(OT - 1, ys[OT - 1])

@@ -20,7 +20,7 @@ GROUPS = 6
 OT = 8
 COLS = PIX * B
 EPS = 1e-5
-PATH = ("tensor", "tensor", "vector", "tensor", "vector", "tensor", "vector", "tensor")
+PATH = ("tensor", "vector", "vector", "vector", "vector", "vector", "tensor", "tensor")
 FLOPS = 2 * C * C3 * COLS + 2 * B * C * C
 
 
@@ -256,13 +256,15 @@ def tile_joint_module_pa_kernel(tc, fv, ft, W1, b1, g1, be1, m1, v1, Wfc1, bfc1,
             yt = pools["back"].tile([P, COLS], F32, tag="yt", bufs=2, align_bytes=64, name="yt%d" % ot)
             nc.vector.transpose(out=yt[:, 0:1024], in_=y[:, 0:1024])
             nc.vector.transpose(out=yt[:, 1024:1152], in_=y[:, 1024:1152])
-            osb = pools["back"].tile([P, P, PIX], F32, tag="osb", bufs=4, name="osbv%d" % ot)
+            ytv = yt[:].rearrange("p (x c) -> p x c", x=PIX)
             nc.vector.tensor_tensor(
-                out=osb[:],
-                in0=yt[:].rearrange("p (x c) -> p c x", x=PIX),
-                in1=gate[:, ot * P : (ot + 1) * P].unsqueeze(2).to_broadcast([P, P, PIX]),
+                out=ytv,
+                in0=ytv,
+                in1=gate[:, ot * P : (ot + 1) * P].unsqueeze(1).to_broadcast([P, PIX, P]),
                 op=ALU.mult,
             )
+            osb = pools["back"].tile([P, P, PIX], F32, tag="osb", bufs=4, name="osbv%d" % ot)
+            nc.scalar.copy(out=osb[:], in_=ytv.rearrange("p x c -> p c x"))
             rows = out_flat.rearrange("(j l) f -> l j f", l=32)
             for i in range(4):
                 f0 = (ot * P + 32 * i) * PIX
@@ -331,6 +333,18 @@ def tile_joint_module_pa_kernel(tc, fv, ft, W1, b1, g1, be1, m1, v1, Wfc1, bfc1,
                         acc = psum.tile([P, 512], F32, tag="bank", name="early")
                         open_acc[(ot, c0)] = acc
                     mx_pass(open_acc[(ot, c0)], ot, g, c0, 512)
+                if g == 3:
+                    for ot in range(4):
+                        gate_transposes(ot)
+                    load_wf(2)
+                    load_wf(3)
+                    for ot in range(4):
+                        gate_tile(ot)
+                if g == 5:
+                    for ot in range(4, OT):
+                        gate_transposes(ot)
+                    for ot in range(4, OT):
+                        gate_tile(ot)
         pools["back"] = ctx.enter_context(tc.tile_pool(name="back", bufs=2))
         ys = {}
         for ot in range(OT):
@@ -346,16 +360,6 @@ def tile_joint_module_pa_kernel(tc, fv, ft, W1, b1, g1, be1, m1, v1, Wfc1, bfc1,
             if ot + 2 < OT:
                 wgr = w_tile(ot + 2)
                 w_quant(ot + 2, wgr)
-            if ot in (2, 3):
-                for i in range(4 * ot - 8, 4 * ot - 4):
-                    gate_transposes(i)
-                if ot == 2:
-                    load_wf(2)
-                    load_wf(3)
-                for i in range(4 * ot - 8, 4 * ot - 4):
-                    gate_tile(i)
-            if ot == 2:
-                finish(0, ys[0])
-            if ot >= 2:
+            if ot >= 1:
                 finish(ot - 1, ys[ot - 1])
         finish(OT - 1, ys[OT - 1])

from contextlib import ExitStack

import concourse.mybir as mybir
from concourse.masks import make_identity

F32 = mybir.dt.float32
BF16 = mybir.dt.bfloat16
U32 = mybir.dt.uint32
U8 = mybir.dt.uint8
FP8X4 = mybir.dt.float8_e4m3fn_x4
ACT = mybir.ActivationFunctionType
ALU = mybir.AluOpType

P = 128
B = 128
C = 1024
C3 = 3072
PIX = 9
GROUPS = 6
OT = 8
COLS = PIX * B
EPS = 1e-5
PATH = ("tensor", "vector", "vector", "vector", "vector", "vector", "tensor", "tensor")
FLOPS = 2 * C * C3 * COLS + 2 * B * C * C


def tile_joint_module_pa_kernel(tc, fv, ft, W1, b1, g1, be1, m1, v1, Wfc1, bfc1, out):
    nc = tc.nc
    with ExitStack() as ctx:
        const = ctx.enter_context(tc.tile_pool(name="const", bufs=1))
        keep = ctx.enter_context(tc.tile_pool(name="keep", bufs=1))
        stage = ctx.enter_context(tc.tile_pool(name="stage", bufs=2))
        psum = ctx.enter_context(tc.psum_pool(name="psum", bufs=8))

        fv_flat = fv.rearrange("b c h w -> b (c h w)")
        out_flat = out.rearrange("b o h w -> b (o h w)")
        wfc_view = Wfc1.rearrange("(t p) k -> p t k", p=P)

        ptile = const.tile([P, P], BF16)
        nc.vector.memset(ptile[:], 0.0)
        bt = const.tile([P, C], BF16)
        nc.vector.memset(bt[:], 0.0)
        ones = const.tile([P, P], BF16)
        nc.vector.memset(ones[:], 1.0)
        for v, vec in enumerate((b1, g1, be1, m1, v1, bfc1)):
            nc.sync.dma_start(out=ptile[8 * v : 8 * v + 8, :], in_=vec.rearrange("(t p) -> t p", p=P))
        nc.scalar.dma_start(out=bt[0:1, :], in_=bfc1.rearrange("(a n) -> a n", a=1))
        ftraw = const.tile([P, C], BF16)
        nc.sync.dma_start(out=ftraw[:], in_=ft)
        warm = const.tile([P, 1], F32)
        nc.vector.memset(warm[:], 1.0)
        nc.scalar.sqrt(out=warm[:], in_=warm[:])
        ident_f = const.tile([P, P], F32)
        make_identity(nc, ident_f[:])
        ident_b = const.tile([P, P], BF16)
        make_identity(nc, ident_b[:])

        fvc = keep.tile([P, GROUPS, COLS], U32, align_bytes=64)
        fvs = keep.tile([P, GROUPS, COLS], U8, align_bytes=64)
        w1c = keep.tile([P, OT, GROUPS * P], U32, align_bytes=64)
        w1s = keep.tile([P, OT, GROUPS * P], U8, align_bytes=64)
        ftT = keep.tile([P, 4 * B], F32)
        gate = keep.tile([P, C], F32, align_bytes=64)
        bp1 = keep.tile([P, OT], F32)

        pools = {}
        fvraw = {}
        wraw = {}
        wfraw = {}

        def load_fv(g):
            raw = pools["front"].tile([P, 512 * PIX], BF16, tag="fvraw", bufs=3, name="fvraw%d" % g)
            nc.sync.dma_start(out=raw[:], in_=fv_flat[:, g * 4608 : (g + 1) * 4608])
            fvraw[g] = raw

        def load_w(ot):
            raw = stage.tile([P, C3], BF16, tag="wraw", bufs=3, name="wraw%d" % ot)
            nc.sync.dma_start(out=raw[:], in_=W1[ot * P : (ot + 1) * P, :])
            wraw[ot] = raw

        def load_wf(i):
            raw = stage.tile([P, 2, C], BF16, tag="wfraw", bufs=2, name="wfraw%d" % i)
            nc.sync.dma_start(out=raw[:], in_=wfc_view[:, 2 * i : 2 * i + 2, :])
            wfraw[i] = raw

        tsbs = {}

        def fv_transposes(g):
            words = fvraw[g][:].bitcast(F32).rearrange("b (u p m) -> b u p m", u=2, p=P, m=PIX)
            tsb = pools["front"].tile([P, 2560], F32, tag="tsb", bufs=2, name="tsb%d" % g)
            tw = tsb[:].rearrange("p (m b u) -> p m b u", m=10, b=B, u=2)
            for m0 in range(0, PIX, 2):
                nm = min(2, PIX - m0)
                bank = psum.tile([P, 2, 2, B], F32, tag="bank", name="fvbank")
                for mm in range(nm):
                    for u in range(2):
                        nc.tensor.transpose(bank[:, mm, u, :], words[:, u, :, m0 + mm], ident_f[:])
                nc.scalar.copy(
                    out=tw[:, m0 : m0 + nm, :, :],
                    in_=bank[:, 0:nm, :, :].rearrange("p m u b -> p m b u"),
                )
            tsbs[g] = tsb

        def fv_regroup(g):
            fb = tsbs[g][:].bitcast(BF16)
            gr = pools["front"].tile([P, PIX * 512], BF16, tag="gr", bufs=2, align_bytes=64, name="gr%d" % g)
            grv = gr[:].rearrange("p (q j a) -> p q j a", q=PIX, j=256, a=2)
            even = (
                fb[:, 0:4098]
                .rearrange("p (a c) -> p a c", a=2)[:, :, 0:2048]
                .rearrange("p a (n j h) -> p a n j h", n=4, j=256, h=2)[:, :, :, :, 0]
                .rearrange("p a n j -> p n j a")
            )
            odd = (
                fb[:, 1:5119]
                .rearrange("p (a c) -> p a c", a=2)[:, :, 0:2048]
                .rearrange("p a (n j h) -> p a n j h", n=4, j=256, h=2)[:, :, :, :, 0]
                .rearrange("p a n j -> p n j a")
            )
            last = (
                fb[:, 512:4610]
                .rearrange("p (a c) -> p a c", a=2)[:, :, 1536:2048]
                .rearrange("p a (j h) -> p a j h", j=256, h=2)[:, :, :, 0]
                .rearrange("p a j -> p j a")
            )
            pairs = grv[:, 0:8, :, :].rearrange("p (n two) j a -> p two n j a", two=2)
            nc.vector.tensor_copy(out=pairs[:, 0, :, :, :], in_=even)
            nc.vector.tensor_copy(out=pairs[:, 1, :, :, :], in_=odd)
            nc.vector.tensor_copy(out=grv[:, 8, :, :], in_=last)
            return gr

        def fv_quant(g, gr):
            nc.vector.quantize_mx(
                out=fvc[:, g, 0:1024].bitcast(FP8X4), scales=fvs[:, g, 0:1024], in_=gr[:, 0:4096]
            )
            nc.vector.quantize_mx(
                out=fvc[:, g, 1024:1152].bitcast(FP8X4), scales=fvs[:, g, 1024:1152], in_=gr[:, 4096:4608]
            )

        def w_tile(ot):
            words = wraw[ot][:].bitcast(F32)
            wgr = stage.tile([P, C3], BF16, tag="wgr", bufs=2, align_bytes=64, name="wgr%d" % ot)
            wv = wgr[:].bitcast(F32).rearrange("p (g o u) -> p g o u", g=GROUPS, o=P, u=2)
            for g0 in range(0, GROUPS, 2):
                bank = psum.tile([P, 2, 2, P], F32, tag="bank", name="wbank")
                for gg in range(2):
                    for u in range(2):
                        k0 = 256 * (g0 + gg) + 128 * u
                        nc.tensor.transpose(bank[:, gg, u, :], words[:, k0 : k0 + 128], ident_f[:])
                nc.scalar.copy(
                    out=wv[:, g0 : g0 + 2, :, :], in_=bank[:].rearrange("p g u o -> p g o u")
                )
            return wgr

        def w_quant(ot, wgr):
            nc.vector.quantize_mx(
                out=w1c[:, ot, 0:512].bitcast(FP8X4), scales=w1s[:, ot, 0:512], in_=wgr[:, 0:2048]
            )
            nc.vector.quantize_mx(
                out=w1c[:, ot, 512:768].bitcast(FP8X4), scales=w1s[:, ot, 512:768], in_=wgr[:, 2048:3072]
            )

        def params():
            pbank = psum.tile([P, P], BF16, tag="bank", name="pbank")
            nc.tensor.transpose(pbank[:], ptile[:], ident_b[:])
            prm = const.tile([P, 48], F32)
            nc.vector.tensor_copy(out=prm[:], in_=pbank[:, 0:48])
            nc.vector.tensor_scalar_add(out=bp1[:], in0=prm[:, 40:48], scalar1=1.0)
            s_t = const.tile([P, OT], F32)
            t_t = const.tile([P, OT], F32)
            tmp = const.tile([P, OT], F32)
            nc.vector.tensor_scalar_add(out=tmp[:], in0=prm[:, 32:40], scalar1=EPS)
            nc.scalar.sqrt(out=tmp[:], in_=tmp[:])
            nc.vector.reciprocal(out=tmp[:], in_=tmp[:])
            nc.vector.tensor_mul(out=s_t[:], in0=prm[:, 8:16], in1=tmp[:])
            nc.vector.tensor_sub(out=t_t[:], in0=prm[:, 0:8], in1=prm[:, 24:32])
            nc.vector.tensor_mul(out=t_t[:], in0=t_t[:], in1=s_t[:])
            nc.vector.tensor_add(out=t_t[:], in0=t_t[:], in1=prm[:, 16:24])
            return s_t, t_t

        def ft_transposes():
            words = ftraw[:].bitcast(F32)
            bank = psum.tile([P, 4, B], F32, tag="bank", name="ftbank")
            for kc in range(4):
                nc.tensor.transpose(bank[:, kc, :], words[:, kc * P : (kc + 1) * P], ident_f[:])
            nc.scalar.copy(out=ftT[:], in_=bank[:].rearrange("p k b -> p (k b)"))

        wfts = {}

        def gate_transposes(ot):
            bank = psum.tile([P, 4, P], F32, tag="bank", name="wfbank")
            words = wfraw[ot // 2][:, ot % 2, :].bitcast(F32)
            for kc in range(4):
                nc.tensor.transpose(bank[:, kc, :], words[:, kc * P : (kc + 1) * P], ident_f[:])
            wft = stage.tile([P, 4 * P], F32, tag="wft", bufs=4, name="wft")
            nc.scalar.copy(out=wft[:], in_=bank[:].rearrange("p k o -> p (k o)"))
            wfts[ot] = wft

        def gate_tile(ot):
            wv = wfts[ot][:].bitcast(BF16).rearrange("p (k o e) -> p k o e", k=4, o=P, e=2)
            fvw = ftT[:].bitcast(BF16).rearrange("p (k b e) -> p k b e", k=4, b=B, e=2)
            cols = slice(ot * P, (ot + 1) * P)
            acc = psum.tile([P, P], F32, tag="bank", name="gbank")
            on_vector = PATH[ot] == "vector"
            for kc in range(4):
                for e in range(2):
                    nc.tensor.matmul(
                        acc[:],
                        lhsT=(wv if on_vector else fvw)[:, kc, :, e],
                        rhs=(fvw if on_vector else wv)[:, kc, :, e],
                        start=(kc == 0 and e == 0),
                        stop=(on_vector and kc == 3 and e == 1),
                    )
            if on_vector:
                gt = stage.tile([P, B], F32, tag="gt", bufs=2, align_bytes=64, name="gt")
                nc.scalar.activation(out=gt[:], in_=acc[:], func=ACT.Identity, bias=bp1[:, ot : ot + 1], scale=1.0)
                nc.vector.transpose(out=gate[:, cols], in_=gt[:])
            else:
                nc.tensor.matmul(acc[:], lhsT=ones[:], rhs=bt[:, cols], start=False, stop=True)
                nc.scalar.activation(out=gate[:, cols], in_=acc[:], func=ACT.Copy, bias=1.0, scale=1.0)

        CHUNKS = ((0, 512), (512, 512), (1024, 128))

        def mx_pass(acc, ot, g, c0, n):
            nc.tensor.matmul_mx(
                out=acc[:],
                lhsT=w1c[:, ot, g * P : (g + 1) * P].bitcast(FP8X4),
                lhsT_scale=w1s[:, ot, g * P : (g + 1) * P],
                rhs=fvc[:, g, c0 : c0 + n].bitcast(FP8X4),
                rhs_scale=fvs[:, g, c0 : c0 + n],
                start=(g == 0),
                stop=(g == GROUPS - 1),
            )

        def bn_relu(y, acc, ot, c0, n, s_t, t_t):
            nc.scalar.activation(
                out=y[:, c0 : c0 + n],
                in_=acc[:],
                func=ACT.Relu,
                bias=t_t[:, ot : ot + 1],
                scale=s_t[:, ot : ot + 1],
            )

        def conv(ot, s_t, t_t, chunks, y):
            for c0, n in chunks:
                acc = psum.tile([P, n], F32, tag="bank", name="acc")
                for g in range(GROUPS):
                    mx_pass(acc, ot, g, c0, n)
                bn_relu(y, acc, ot, c0, n, s_t, t_t)

        def new_y(ot):
            y = pools["back"].tile([P, COLS], F32, tag="y", bufs=3, align_bytes=64, name="y%d" % ot)
            return y

        def finish_on_vector(ot, y):
            yt = pools["back"].tile([P, COLS], F32, tag="yt", bufs=2, align_bytes=64, name="yt%d" % ot)
            nc.vector.transpose(out=yt[:, 0:1024], in_=y[:, 0:1024])
            nc.vector.transpose(out=yt[:, 1024:1152], in_=y[:, 1024:1152])
            ytv = yt[:].rearrange("p (x c) -> p x c", x=PIX)
            nc.vector.tensor_tensor(
                out=ytv,
                in0=ytv,
                in1=gate[:, ot * P : (ot + 1) * P].unsqueeze(1).to_broadcast([P, PIX, P]),
                op=ALU.mult,
            )
            osb = pools["back"].tile([P, P, PIX], F32, tag="osb", bufs=4, name="osbv%d" % ot)
            nc.scalar.copy(out=osb[:], in_=ytv.rearrange("p x c -> p c x"))
            rows = out_flat.rearrange("(j l) f -> l j f", l=32)
            for i in range(4):
                f0 = (ot * P + 32 * i) * PIX
                nc.sync.dma_start(
                    out=rows[:, :, f0 : f0 + 32 * PIX],
                    in_=osb[32 * i : 32 * i + 32, :, :].rearrange("l (j o) x -> l j (o x)", j=4),
                )

        def finish(ot, y):
            if PATH[ot] == "vector":
                finish_on_vector(ot, y)
                return
            planes = pools["back"].tile([P, PIX, P], F32, tag="planes", bufs=3, name="planes%d" % ot)
            for x0 in range(0, PIX, 4):
                nx = min(4, PIX - x0)
                z = psum.tile([P, nx, P], F32, tag="bank", name="z")
                for i in range(nx):
                    q = x0 + i
                    nc.tensor.transpose(z[:, i, :], y[:, q * B : (q + 1) * B], ident_f[:])
                nc.scalar.copy(out=planes[:, x0 : x0 + nx, :], in_=z[:])
            step = 64 if ot == OT - 1 else P
            for i0 in range(0, P, step):
                osb = pools["back"].tile([P, step, PIX], F32, tag="osb", bufs=4, name="osb%d" % ot)
                o0 = ot * P + i0
                nc.vector.tensor_tensor(
                    out=osb[:],
                    in0=planes[:, :, i0 : i0 + step].rearrange("b x o -> b o x"),
                    in1=gate[:, o0 : o0 + step].unsqueeze(2).to_broadcast([P, step, PIX]),
                    op=ALU.mult,
                )
                nc.sync.dma_start(
                    out=out_flat[:, o0 * PIX : (o0 + step) * PIX], in_=osb[:].rearrange("b o x -> b (o x)")
                )

        EARLY = ((0, 0), (0, 512), (1, 0), (1, 512))
        with tc.tile_pool(name="front", bufs=2) as front:
            pools["front"] = front
            load_w(0)
            load_fv(0)
            load_w(1)
            load_fv(1)
            load_fv(2)
            s_t, t_t = params()
            ft_transposes()
            wgrs = {0: w_tile(0)}
            fv_transposes(0)
            w_quant(0, wgrs[0])
            wgrs[1] = w_tile(1)
            fv_transposes(1)
            grs = {0: fv_regroup(0)}
            open_acc = {}
            extra = {0: lambda: load_w(2), 1: lambda: load_wf(0), 2: lambda: load_wf(1)}
            for g in range(GROUPS):
                if g + 3 < GROUPS:
                    load_fv(g + 3)
                    extra[g]()
                if g + 2 < GROUPS:
                    fv_transposes(g + 2)
                if g + 1 < GROUPS:
                    grs[g + 1] = fv_regroup(g + 1)
                fv_quant(g, grs[g])
                if g == 0:
                    w_quant(1, wgrs[1])
                for ot, c0 in EARLY:
                    if g == 0:
                        acc = psum.tile([P, 512], F32, tag="bank", name="early")
                        open_acc[(ot, c0)] = acc
                    mx_pass(open_acc[(ot, c0)], ot, g, c0, 512)
                if g == 3:
                    for ot in range(4):
                        gate_transposes(ot)
                    load_wf(2)
                    load_wf(3)
                    for ot in range(4):
                        gate_tile(ot)
                if g == 5:
                    for ot in range(4, OT):
                        gate_transposes(ot)
                    for ot in range(4, OT):
                        gate_tile(ot)
        pools["back"] = ctx.enter_context(tc.tile_pool(name="back", bufs=2))
        ys = {}
        for ot in range(OT):
            ys[ot] = new_y(ot)
            if ot < 2:
                bn_relu(ys[ot], open_acc[(ot, 0)], ot, 0, 512, s_t, t_t)
                bn_relu(ys[ot], open_acc[(ot, 512)], ot, 512, 512, s_t, t_t)
                conv(ot, s_t, t_t, CHUNKS[2:], ys[ot])
            else:
                conv(ot, s_t, t_t, CHUNKS, ys[ot])
            if ot + 3 < OT:
                load_w(ot + 3)
            if ot + 2 < OT:
                wgr = w_tile(ot + 2)
                w_quant(ot + 2, wgr)
            if ot >= 1:
                finish(ot - 1, ys[ot - 1])
        finish(OT - 1, ys[OT - 1])
